import numpy as np
import ml_dtypes


def mxq(x, axis, fmt="e4m3"):
    dtype, down = {"e4m3": (ml_dtypes.float8_e4m3fn, 7), "e5m2": (ml_dtypes.float8_e5m2, 14)}[fmt]
    v = np.moveaxis(np.asarray(x, np.float32).astype(ml_dtypes.bfloat16).astype(np.float64), axis, -1)
    blocks = v.reshape(v.shape[:-1] + (-1, 32))
    amax = np.abs(blocks).max(-1, keepdims=True)
    byte = np.maximum(np.where(amax > 0, np.frexp(amax)[1] - 1 + 127, 0) - down, 1)
    scale = np.exp2(byte - 127.0)
    codes = (blocks / scale).astype(np.float32).astype(dtype).astype(np.float64)
    return np.moveaxis((codes * scale).reshape(v.shape), -1, axis)


WIDE = False


def mx_kscale(k):
    if not WIDE:
        return np.ones(k)
    levels = np.array([10, -10, 5, -5, 0])
    a = np.random.permutation(np.resize(levels, k // 512 * 4)).reshape(k // 512, 4)
    idx = np.arange(k)
    return np.exp2(a[idx // 512, idx % 128 // 32])


BF16 = ml_dtypes.bfloat16


def bf(x):
    return np.asarray(x, np.float32).astype(BF16)


def f64(x):
    return np.asarray(x).astype(np.float64)


B, C_IN, C_OUT, HEADS, H, W = 8, 1024, 256, 2, 16, 32
DH = C_OUT // HEADS
M = H * W


def setup_inputs():
    s = mx_kscale(C_IN)
    return {
        "vh": bf(np.random.standard_normal((B, HEADS, DH, M)) * 2.0),
        "zh": bf(np.random.standard_normal((B, HEADS, DH, M))),
        "r_pos": bf(np.random.standard_normal((HEADS, DH, M)) * np.sqrt(0.5)),
        "x": bf(np.random.standard_normal((B, C_IN, H, W)) * s[None, :, None, None]),
        "w_q": bf(np.random.standard_normal((C_OUT, C_IN)) * 2.0 / np.sqrt(C_IN) / s[None, :]),
    }


def reference(vh, zh, r_pos, x, w_q):
    vt = f64(vh).transpose(0, 1, 3, 2)
    scores = vt @ f64(zh) + vt @ f64(r_pos)
    sc = scores / np.sqrt(DH)
    e = np.exp(sc - sc.max(-1, keepdims=True))
    xf = f64(x).reshape(B, C_IN, M)
    qh = (mxq(f64(w_q), 1, "e4m3") @ mxq(xf, 1, "e4m3")).reshape(B, HEADS, DH, M)
    o = (mxq(e, 3, "e4m3") @ mxq(qh, 3, "e4m3").transpose(0, 1, 3, 2)) / e.sum(-1, keepdims=True)
    return o.transpose(0, 1, 3, 2).reshape(B, C_OUT, H, W)

@@ -1,0 +1,312 @@
+from contextlib import ExitStack
+import math
+
+import concourse.mybir as mybir
+from concourse.masks import make_identity
+
+F32 = mybir.dt.float32
+BF16 = mybir.dt.bfloat16
+U32 = mybir.dt.uint32
+U8 = mybir.dt.uint8
+FP8X4 = mybir.dt.float8_e4m3fn_x4
+ALU = mybir.AluOpType
+FUNC = mybir.ActivationFunctionType
+AXIS = mybir.AxisListType
+
+P = 128
+PACK = 4
+K_PASS = P * PACK
+
+BATCH = 8
+HEADS = 2
+DH = 128
+PIXELS = 512
+C_IN = 1024
+PASSES = C_IN // K_PASS
+UNITS = BATCH * HEADS
+TILES_PER_UNIT = PIXELS // P
+TILES = UNITS * TILES_PER_UNIT
+SCALE = 1.0 / math.sqrt(DH)
+
+FLOPS = 2 * BATCH * HEADS * DH * C_IN * PIXELS + 3 * 2 * UNITS * PIXELS * PIXELS * DH
+
+E_TRANSPOSE = 3
+X_QUANTISE = 6
+QUANTISE_E = 12
+PROJECT = 12
+Q_OUT = 13
+QUANTISE_Q = 15
+ATTEND = 19
+NORMALISE = 21
+O_TRANSPOSE = 25
+W_TICK = 6
+LAST_TICK = TILES_PER_UNIT * (UNITS - 1) + O_TRANSPOSE
+
+
+def due(k, lag, count):
+    i, phase = divmod(k - lag, TILES_PER_UNIT)
+    if phase == 0 and 0 <= i < count:
+        return i
+    return None
+
+
+def tile_multiheadselfattention2d_pa_t_kernel(tc, vh, zh, r_pos, x, w_q, out):
+    nc = tc.nc
+    with ExitStack() as ctx:
+        const = ctx.enter_context(tc.tile_pool(name="const", bufs=1))
+        inputs = ctx.enter_context(tc.tile_pool(name="inputs", bufs=BATCH))
+        work = ctx.enter_context(tc.tile_pool(name="work", bufs=2))
+        psum_s = ctx.enter_context(tc.psum_pool(name="psum_s", bufs=3))
+        psum_t = ctx.enter_context(tc.psum_pool(name="psum_t", bufs=2))
+        psum_mx = ctx.enter_context(tc.psum_pool(name="psum_mx", bufs=2))
+        psum_o = ctx.enter_context(tc.psum_pool(name="psum_o", bufs=1))
+
+        v_sb = []
+        z_sb = []
+        x_sb = []
+        r_sb = const.tile([P, HEADS, PIXELS], BF16, name="r_sb")
+        w_sb = const.tile([P, HEADS, C_IN], BF16, name="w_sb")
+        for b in range(BATCH):
+            v_sb.append(inputs.tile([P, HEADS, PIXELS], BF16, name="v_sb"))
+            z_sb.append(inputs.tile([P, HEADS, PIXELS], BF16, name="z_sb"))
+            x_sb.append(inputs.tile([P, PASSES, PACK, PIXELS], BF16, name="x_sb"))
+            nc.sync.dma_start(out=v_sb[b][:], in_=vh[b].rearrange("h d m -> d h m"))
+            nc.sync.dma_start(out=z_sb[b][:], in_=zh[b].rearrange("h d n -> d h n"))
+            if b == 0:
+                nc.sync.dma_start(out=r_sb[:], in_=r_pos.rearrange("h d n -> d h n"))
+            for g in range(PASSES):
+                nc.sync.dma_start(
+                    out=x_sb[b][:, g],
+                    in_=x[b, g * K_PASS : (g + 1) * K_PASS].rearrange("(p j) y x -> p j (y x)", j=PACK),
+                )
+            if b == 0:
+                nc.sync.dma_start(out=w_sb[:], in_=w_q.rearrange("(h c) k -> c h k", h=HEADS))
+
+        ident_bf = const.tile([P, P], BF16, name="ident_bf")
+        make_identity(nc, ident_bf[:])
+        ident_f32 = const.tile([P, P], F32, name="ident_f32")
+        make_identity(nc, ident_f32[:])
+
+        w_pairs = const.tile([P, PASSES, HEADS, DH, 2], F32, name="w_pairs", align_bytes=64)
+        w_codes = const.tile([P, PASSES, HEADS, DH], U32, name="w_codes", align_bytes=64)
+        w_scales = const.tile([P, PASSES, HEADS, DH], U8, name="w_scales", align_bytes=64)
+
+        s_ps = {}
+        neg_max = {}
+        e_sb = {}
+        e_t = {}
+        e_grouped = {}
+        e_codes = {}
+        e_scales = {}
+        row_sum = {}
+        x_grouped = {}
+        x_codes = {}
+        x_scales = {}
+        q_ps = {}
+        q_grouped = {}
+        q_codes = {}
+        q_scales = {}
+        o_ps = {}
+        o_sb = {}
+        o_t = {}
+
+        def prepare_weights():
+            for h in range(HEADS):
+                words = w_sb[:, h, :].bitcast(F32).rearrange("c (g p u) -> c g u p", g=PASSES, u=2)
+                w_t = psum_mx.tile([P, PASSES, 2, DH], F32, name="w_t", tag="mx")
+                for g in range(PASSES):
+                    for u in range(2):
+                        nc.tensor.transpose(out=w_t[:, g, u, :], in_=words[:, g, u, :], identity=ident_f32[:])
+                nc.vector.tensor_copy(out=w_pairs[:, :, h, :, :], in_=w_t[:].rearrange("p g u c -> p g c u"))
+
+        def quantise_w():
+            nc.vector.quantize_mx(
+                out=w_codes[:].rearrange("p g h c -> p (g h c)").bitcast(FP8X4),
+                scales=w_scales[:].rearrange("p g h c -> p (g h c)"),
+                in_=w_pairs[:].rearrange("p g h c u -> p (g h c u)").bitcast(BF16),
+            )
+
+        def score_matmuls(k):
+            u, mt = divmod(k, TILES_PER_UNIT)
+            b, h = divmod(u, HEADS)
+            s_ps[k] = psum_s.tile([P, PIXELS], F32, name="s_ps", tag="s")
+            queries = v_sb[b][:, h, mt * P : (mt + 1) * P]
+            nc.tensor.matmul(out=s_ps[k][:], lhsT=queries, rhs=z_sb[b][:, h, :], start=True, stop=False)
+            nc.tensor.matmul(out=s_ps[k][:], lhsT=queries, rhs=r_sb[:, h, :], start=False, stop=True)
+
+        def row_maximum(k):
+            row_max = work.tile([P, 1], F32, name="row_max", bufs=4)
+            nc.vector.tensor_reduce(out=row_max[:], in_=s_ps[k][:], axis=AXIS.X, op=ALU.max)
+            neg_max[k] = work.tile([P, 1], F32, name="neg_max", bufs=4)
+            nc.vector.tensor_scalar_mul(out=neg_max[k][:], in0=row_max[:], scalar1=-SCALE)
+
+        def exponentials(k):
+            u, mt = divmod(k, TILES_PER_UNIT)
+            if mt == 0:
+                row_sum[u] = work.tile([P, TILES_PER_UNIT], F32, name="row_sum", bufs=8)
+            e_sb[k] = work.tile([P, PIXELS], BF16, name="e_sb", bufs=6)
+            nc.scalar.activation(
+                out=e_sb[k][:],
+                in_=s_ps[k][:],
+                func=FUNC.Exp,
+                bias=neg_max[k][:],
+                scale=SCALE,
+                accum_out=row_sum[u][:, mt : mt + 1],
+            )
+
+        def transpose_e(k):
+            pair, a = divmod(k, 2)
+            if a == 0:
+                e_t[pair] = psum_t.tile([P, 2, PACK, P], BF16, name="e_t", tag="e_t")
+            for t in range(PACK):
+                nc.tensor.transpose(out=e_t[pair][:, a, t, :], in_=e_sb[k][:, t * P : (t + 1) * P], identity=ident_bf[:])
+
+        def group_e(pair):
+            u, half = divmod(pair, 2)
+            if half == 0:
+                e_grouped[u] = work.tile([P, PIXELS, PACK], BF16, name="e_grouped", bufs=4, align_bytes=64)
+            nc.scalar.copy(
+                out=e_grouped[u][:, half * 2 * P : (half + 1) * 2 * P, :].rearrange("p (a r) t -> p a r t", a=2),
+                in_=e_t[pair][:].rearrange("p a t r -> p a r t"),
+            )
+
+        def quantise_e(u):
+            e_codes[u] = work.tile([P, PIXELS], U32, name="e_codes", bufs=4, align_bytes=64)
+            e_scales[u] = work.tile([P, PIXELS], U8, name="e_scales", bufs=4, align_bytes=64)
+            nc.vector.quantize_mx(
+                out=e_codes[u][:].bitcast(FP8X4),
+                scales=e_scales[u][:],
+                in_=e_grouped[u][:].rearrange("p m t -> p (m t)"),
+            )
+
+        def group_x(piece):
+            half_image, quarter = divmod(piece, TILES_PER_UNIT)
+            b, g = divmod(half_image, PASSES)
+            if quarter == 0:
+                x_grouped[half_image] = work.tile([P, PIXELS, PACK], BF16, name="x_grouped", bufs=3, align_bytes=64)
+            cols = slice(quarter * P, (quarter + 1) * P)
+            nc.vector.tensor_copy(
+                out=x_grouped[half_image][:, cols, :].rearrange("p (c i) j -> p c j i", i=4),
+                in_=x_sb[b][:, g, :, cols].rearrange("p j (c i) -> p c j i", i=4),
+            )
+
+        def quantise_x(half_image):
+            b, g = divmod(half_image, PASSES)
+            if g == 0:
+                x_codes[b] = work.tile([P, PASSES, PIXELS], U32, name="x_codes", bufs=3, align_bytes=64)
+                x_scales[b] = work.tile([P, PASSES, PIXELS], U8, name="x_scales", bufs=3, align_bytes=64)
+            nc.vector.quantize_mx(
+                out=x_codes[b][:, g, :].bitcast(FP8X4),
+                scales=x_scales[b][:, g, :],
+                in_=x_grouped[half_image][:].rearrange("p n j -> p (n j)"),
+            )
+
+        def project(u):
+            b, h = divmod(u, HEADS)
+            q_ps[u] = psum_mx.tile([P, PACK, DH], F32, name="q_ps", tag="mx")
+            for t in range(PACK):
+                for g in range(PASSES):
+                    nc.tensor.matmul_mx(
+                        out=q_ps[u][:, t, :],
+                        lhsT=x_codes[b][:, g, t * P : (t + 1) * P].bitcast(FP8X4),
+                        lhsT_scale=x_scales[b][:, g, t * P : (t + 1) * P],
+                        rhs=w_codes[:, g, h, :].bitcast(FP8X4),
+                        rhs_scale=w_scales[:, g, h, :],
+                        start=(g == 0),
+                        stop=(g == PASSES - 1),
+                    )
+
+        def group_q(u):
+            q_grouped[u] = work.tile([P, DH, PACK], BF16, name="q_grouped", bufs=2, align_bytes=64)
+            nc.scalar.copy(out=q_grouped[u][:], in_=q_ps[u][:].rearrange("p t d -> p d t"))
+
+        def quantise_q(u):
+            q_codes[u] = work.tile([P, DH], U32, name="q_codes", bufs=3, align_bytes=64)
+            q_scales[u] = work.tile([P, DH], U8, name="q_scales", bufs=3, align_bytes=64)
+            nc.vector.quantize_mx(
+                out=q_codes[u][:].bitcast(FP8X4),
+                scales=q_scales[u][:],
+                in_=q_grouped[u][:].rearrange("p d t -> p (d t)"),
+            )
+
+        def attend(u):
+            o_ps[u] = psum_mx.tile([P, TILES_PER_UNIT, DH], F32, name="o_ps", tag="mx")
+            for mt in range(TILES_PER_UNIT):
+                nc.tensor.matmul_mx(
+                    out=o_ps[u][:, mt, :],
+                    lhsT=e_codes[u][:, mt * P : (mt + 1) * P].bitcast(FP8X4),
+                    lhsT_scale=e_scales[u][:, mt * P : (mt + 1) * P],
+                    rhs=q_codes[u][:].bitcast(FP8X4),
+                    rhs_scale=q_scales[u][:],
+                    start=True,
+                    stop=True,
+                )
+
+        def normalise(u):
+            inverse = work.tile([P, TILES_PER_UNIT], F32, name="inverse", bufs=2)
+            nc.vector.reciprocal(out=inverse[:], in_=row_sum[u][:])
+            o_sb[u] = work.tile([P, TILES_PER_UNIT, DH], F32, name="o_sb", bufs=3)
+            nc.vector.tensor_tensor(
+                out=o_sb[u][:],
+                in0=o_ps[u][:],
+                in1=inverse[:].unsqueeze(2).to_broadcast([P, TILES_PER_UNIT, DH]),
+                op=ALU.mult,
+            )
+
+        def transpose_o(u):
+            o_t[u] = psum_o.tile([P, TILES_PER_UNIT, P], F32, name="o_t", tag="o_t")
+            for mt in range(TILES_PER_UNIT):
+                nc.tensor.transpose(out=o_t[u][:, mt, :], in_=o_sb[u][:, mt, :], identity=ident_f32[:])
+
+        def store(u):
+            b, h = divmod(u, HEADS)
+            result = work.tile([P, PIXELS], F32, name="result", bufs=4)
+            nc.scalar.copy(out=result[:], in_=o_t[u][:].rearrange("d mt m -> d (mt m)"))
+            nc.sync.dma_start(out=out[b, h * DH : (h + 1) * DH].rearrange("c y x -> c (y x)"), in_=result[:])
+
+        with tc.manual_schedule():
+            for k in range(LAST_TICK + 1):
+                if k < TILES:
+                    score_matmuls(k)
+                if 0 <= k - E_TRANSPOSE < TILES:
+                    transpose_e(k - E_TRANSPOSE)
+                u = due(k, O_TRANSPOSE, UNITS)
+                if u is not None:
+                    transpose_o(u)
+                if k == W_TICK:
+                    prepare_weights()
+                u = due(k, ATTEND, UNITS)
+                if u is not None:
+                    attend(u)
+                u = due(k, PROJECT, UNITS)
+                if u is not None:
+                    project(u)
+
+                if k < TILES:
+                    row_maximum(k)
+                    group_x(k)
+                if k == W_TICK + 1:
+                    quantise_w()
+                i = due(k, X_QUANTISE, BATCH * PASSES)
+                if i is not None:
+                    quantise_x(i)
+                u = due(k, QUANTISE_Q, UNITS)
+                if u is not None:
+                    quantise_q(u)
+                u = due(k, NORMALISE, UNITS)
+                if u is not None:
+                    normalise(u)
+                u = due(k, QUANTISE_E, UNITS)
+                if u is not None:
+                    quantise_e(u)
+
+                if k < TILES:
+                    exponentials(k)
+                if 0 <= k - E_TRANSPOSE < TILES and (k - E_TRANSPOSE) % 2 == 1:
+                    group_e((k - E_TRANSPOSE) // 2)
+                u = due(k, Q_OUT, UNITS)
+                if u is not None:
+                    group_q(u)
+                u = due(k, O_TRANSPOSE, UNITS)
+                if u is not None:
+                    store(u)

@@ -11,7 +11,6 @@ U8 = mybir.dt.uint8
 FP8X4 = mybir.dt.float8_e4m3fn_x4
 ALU = mybir.AluOpType
 FUNC = mybir.ActivationFunctionType
-AXIS = mybir.AxisListType
 
 P = 128
 PACK = 4
@@ -70,14 +69,14 @@ def tile_multiheadselfattention2d_pa_t_kernel(tc, vh, zh, r_pos, x, w_q, out):
             v_sb.append(inputs.tile([P, HEADS, PIXELS], BF16, name="v_sb"))
             z_sb.append(inputs.tile([P, HEADS, PIXELS], BF16, name="z_sb"))
             x_sb.append(inputs.tile([P, PASSES, PACK, PIXELS], BF16, name="x_sb"))
-            nc.sync.dma_start(out=v_sb[b][:], in_=vh[b].rearrange("h d m -> d h m"))
-            nc.sync.dma_start(out=z_sb[b][:], in_=zh[b].rearrange("h d n -> d h n"))
-            if b == 0:
-                nc.sync.dma_start(out=r_sb[:], in_=r_pos.rearrange("h d n -> d h n"))
-            for g in range(PASSES):
+            for h in range(HEADS):
+                nc.sync.dma_start(out=v_sb[b][:, h, :], in_=vh[b, h])
+                nc.sync.dma_start(out=z_sb[b][:, h, :], in_=zh[b, h])
+                if b == 0:
+                    nc.sync.dma_start(out=r_sb[:, h, :], in_=r_pos[h])
                 nc.sync.dma_start(
-                    out=x_sb[b][:, g],
-                    in_=x[b, g * K_PASS : (g + 1) * K_PASS].rearrange("(p j) y x -> p j (y x)", j=PACK),
+                    out=x_sb[b][:, h],
+                    in_=x[b, h * K_PASS : (h + 1) * K_PASS].rearrange("(p j) y x -> p j (y x)", j=PACK),
                 )
             if b == 0:
                 nc.sync.dma_start(out=w_sb[:], in_=w_q.rearrange("(h c) k -> c h k", h=HEADS))
@@ -92,6 +91,7 @@ def tile_multiheadselfattention2d_pa_t_kernel(tc, vh, zh, r_pos, x, w_q, out):
         w_scales = const.tile([P, PASSES, HEADS, DH], U8, name="w_scales", align_bytes=64)
 
         s_ps = {}
+        neg_s = {}
         neg_max = {}
         e_sb = {}
         e_t = {}
@@ -135,10 +135,17 @@ def tile_multiheadselfattention2d_pa_t_kernel(tc, vh, zh, r_pos, x, w_q, out):
             nc.tensor.matmul(out=s_ps[k][:], lhsT=queries, rhs=r_sb[:, h, :], start=False, stop=True)
 
         def row_maximum(k):
-            row_max = work.tile([P, 1], F32, name="row_max", bufs=4)
-            nc.vector.tensor_reduce(out=row_max[:], in_=s_ps[k][:], axis=AXIS.X, op=ALU.max)
-            neg_max[k] = work.tile([P, 1], F32, name="neg_max", bufs=4)
-            nc.vector.tensor_scalar_mul(out=neg_max[k][:], in0=row_max[:], scalar1=-SCALE)
+            neg_s[k] = work.tile([P, PIXELS], F32, name="neg_s", bufs=6)
+            neg_max[k] = work.tile([P, 1], F32, name="neg_max", bufs=8)
+            nc.vector.tensor_scalar(
+                out=neg_s[k][:],
+                in0=s_ps[k][:],
+                scalar1=-SCALE,
+                scalar2=None,
+                op0=ALU.mult,
+                op1=ALU.min,
+                accum_out=neg_max[k][:],
+            )
 
         def exponentials(k):
             u, mt = divmod(k, TILES_PER_UNIT)
@@ -147,10 +154,10 @@ def tile_multiheadselfattention2d_pa_t_kernel(tc, vh, zh, r_pos, x, w_q, out):
             e_sb[k] = work.tile([P, PIXELS], BF16, name="e_sb", bufs=6)
             nc.scalar.activation(
                 out=e_sb[k][:],
-                in_=s_ps[k][:],
+                in_=neg_s[k][:],
                 func=FUNC.Exp,
                 bias=neg_max[k][:],
-                scale=SCALE,
+                scale=-1.0,
                 accum_out=row_sum[u][:, mt : mt + 1],
             )
 

@@ -81,8 +81,6 @@ def tile_multiheadselfattention2d_pa_t_kernel(tc, vh, zh, r_pos, x, w_q, out):
             if b == 0:
                 nc.sync.dma_start(out=w_sb[:], in_=w_q.rearrange("(h c) k -> c h k", h=HEADS))
 
-        ident_bf = const.tile([P, P], BF16, name="ident_bf")
-        make_identity(nc, ident_bf[:])
         ident_f32 = const.tile([P, P], F32, name="ident_f32")
         make_identity(nc, ident_f32[:])
 
@@ -153,8 +151,8 @@ def tile_multiheadselfattention2d_pa_t_kernel(tc, vh, zh, r_pos, x, w_q, out):
                 row_sum[u] = work.tile([P, TILES_PER_UNIT], F32, name="row_sum", bufs=8)
             e_sb[k] = work.tile([P, PIXELS], BF16, name="e_sb", bufs=6)
             nc.scalar.activation(
-                out=e_sb[k][:],
-                in_=neg_s[k][:],
+                out=e_sb[k][:].rearrange("m (u p e) -> m u p e", u=2, e=2),
+                in_=neg_s[k][:].rearrange("m (u e p) -> m u p e", u=2, e=2),
                 func=FUNC.Exp,
                 bias=neg_max[k][:],
                 scale=-1.0,
@@ -164,17 +162,18 @@ def tile_multiheadselfattention2d_pa_t_kernel(tc, vh, zh, r_pos, x, w_q, out):
         def transpose_e(k):
             pair, a = divmod(k, 2)
             if a == 0:
-                e_t[pair] = psum_t.tile([P, 2, PACK, P], BF16, name="e_t", tag="e_t")
-            for t in range(PACK):
-                nc.tensor.transpose(out=e_t[pair][:, a, t, :], in_=e_sb[k][:, t * P : (t + 1) * P], identity=ident_bf[:])
+                e_t[pair] = psum_t.tile([P, 2, 2, P], F32, name="e_t", tag="e_t")
+            words = e_sb[k][:].bitcast(F32)
+            for u in range(2):
+                nc.tensor.transpose(out=e_t[pair][:, a, u, :], in_=words[:, u * P : (u + 1) * P], identity=ident_f32[:])
 
         def group_e(pair):
             u, half = divmod(pair, 2)
             if half == 0:
-                e_grouped[u] = work.tile([P, PIXELS, PACK], BF16, name="e_grouped", bufs=4, align_bytes=64)
+                e_grouped[u] = work.tile([P, PIXELS, 2], F32, name="e_grouped", bufs=4, align_bytes=64)
             nc.scalar.copy(
-                out=e_grouped[u][:, half * 2 * P : (half + 1) * 2 * P, :].rearrange("p (a r) t -> p a r t", a=2),
-                in_=e_t[pair][:].rearrange("p a t r -> p a r t"),
+                out=e_grouped[u][:, half * 2 * P : (half + 1) * 2 * P, :].rearrange("p (a r) w -> p a r w", a=2),
+                in_=e_t[pair][:].rearrange("p a w r -> p a r w"),
             )
 
         def quantise_e(u):
@@ -183,7 +182,7 @@ def tile_multiheadselfattention2d_pa_t_kernel(tc, vh, zh, r_pos, x, w_q, out):
             nc.vector.quantize_mx(
                 out=e_codes[u][:].bitcast(FP8X4),
                 scales=e_scales[u][:],
-                in_=e_grouped[u][:].rearrange("p m t -> p (m t)"),
+                in_=e_grouped[u][:].rearrange("p m w -> p (m w)").bitcast(BF16),
             )
 
         def group_x(piece):

@@ -29,17 +29,17 @@ SCALE = 1.0 / math.sqrt(DH)
 
 FLOPS = 2 * BATCH * HEADS * DH * C_IN * PIXELS + 3 * 2 * UNITS * PIXELS * PIXELS * DH
 
-E_TRANSPOSE = 3
-X_QUANTISE = 6
-QUANTISE_E = 12
-PROJECT = 12
-Q_OUT = 13
-QUANTISE_Q = 15
-ATTEND = 19
-NORMALISE = 21
-O_TRANSPOSE = 25
+E_TRANSPOSE = 5
+X_FIRST = 3
+PROJECT = 9
+Q_OUT = 10
+INVERT = 10
+SPREAD = 11
+QUANTISE = 12
+ATTEND = 13
+NORMALISE = 15
 W_TICK = 6
-LAST_TICK = TILES_PER_UNIT * (UNITS - 1) + O_TRANSPOSE
+LAST_TICK = TILES_PER_UNIT * (UNITS - 1) + NORMALISE
 
 
 def due(k, lag, count):
@@ -104,9 +104,9 @@ def tile_multiheadselfattention2d_pa_t_kernel(tc, vh, zh, r_pos, x, w_q, out):
         q_grouped = {}
         q_codes = {}
         q_scales = {}
+        inverse = {}
+        spread = {}
         o_ps = {}
-        o_sb = {}
-        o_t = {}
 
         def prepare_weights():
             for h in range(HEADS):
@@ -133,8 +133,8 @@ def tile_multiheadselfattention2d_pa_t_kernel(tc, vh, zh, r_pos, x, w_q, out):
             nc.tensor.matmul(out=s_ps[k][:], lhsT=queries, rhs=r_sb[:, h, :], start=False, stop=True)
 
         def row_maximum(k):
-            neg_s[k] = work.tile([P, PIXELS], F32, name="neg_s", bufs=6)
-            neg_max[k] = work.tile([P, 1], F32, name="neg_max", bufs=8)
+            neg_s[k] = work.tile([P, PIXELS], F32, name="neg_s", bufs=8)
+            neg_max[k] = work.tile([P, 1], F32, name="neg_max", bufs=10)
             nc.vector.tensor_scalar(
                 out=neg_s[k][:],
                 in0=s_ps[k][:],
@@ -149,7 +149,7 @@ def tile_multiheadselfattention2d_pa_t_kernel(tc, vh, zh, r_pos, x, w_q, out):
             u, mt = divmod(k, TILES_PER_UNIT)
             if mt == 0:
                 row_sum[u] = work.tile([P, TILES_PER_UNIT], F32, name="row_sum", bufs=8)
-            e_sb[k] = work.tile([P, PIXELS], BF16, name="e_sb", bufs=6)
+            e_sb[k] = work.tile([P, PIXELS], BF16, name="e_sb", bufs=8)
             nc.scalar.activation(
                 out=e_sb[k][:].rearrange("m (u p e) -> m u p e", u=2, e=2),
                 in_=neg_s[k][:].rearrange("m (u e p) -> m u p e", u=2, e=2),
@@ -185,15 +185,16 @@ def tile_multiheadselfattention2d_pa_t_kernel(tc, vh, zh, r_pos, x, w_q, out):
                 in_=e_grouped[u][:].rearrange("p m w -> p (m w)").bitcast(BF16),
             )
 
-        def group_x(piece):
-            half_image, quarter = divmod(piece, TILES_PER_UNIT)
+        def group_x(half_image):
             b, g = divmod(half_image, PASSES)
-            if quarter == 0:
-                x_grouped[half_image] = work.tile([P, PIXELS, PACK], BF16, name="x_grouped", bufs=3, align_bytes=64)
-            cols = slice(quarter * P, (quarter + 1) * P)
-            nc.vector.tensor_copy(
-                out=x_grouped[half_image][:, cols, :].rearrange("p (c i) j -> p c j i", i=4),
-                in_=x_sb[b][:, g, :, cols].rearrange("p j (c i) -> p c j i", i=4),
+            x_grouped[half_image] = work.tile([P, PIXELS, PACK], BF16, name="x_grouped", bufs=1, align_bytes=64)
+            nc.gpsimd.tensor_scalar(
+                out=x_grouped[half_image][:],
+                in0=x_sb[b][:, g].rearrange("p j n -> p n j"),
+                scalar1=1.0,
+                scalar2=0.0,
+                op0=ALU.mult,
+                op1=ALU.add,
             )
 
         def quantise_x(half_image):
@@ -236,49 +237,54 @@ def tile_multiheadselfattention2d_pa_t_kernel(tc, vh, zh, r_pos, x, w_q, out):
             )
 
         def attend(u):
-            o_ps[u] = psum_mx.tile([P, TILES_PER_UNIT, DH], F32, name="o_ps", tag="mx")
-            for mt in range(TILES_PER_UNIT):
-                nc.tensor.matmul_mx(
-                    out=o_ps[u][:, mt, :],
-                    lhsT=e_codes[u][:, mt * P : (mt + 1) * P].bitcast(FP8X4),
-                    lhsT_scale=e_scales[u][:, mt * P : (mt + 1) * P],
-                    rhs=q_codes[u][:].bitcast(FP8X4),
-                    rhs_scale=q_scales[u][:],
-                    start=True,
-                    stop=True,
-                )
-
-        def normalise(u):
-            inverse = work.tile([P, TILES_PER_UNIT], F32, name="inverse", bufs=2)
-            nc.vector.reciprocal(out=inverse[:], in_=row_sum[u][:])
-            o_sb[u] = work.tile([P, TILES_PER_UNIT, DH], F32, name="o_sb", bufs=3)
-            nc.vector.tensor_tensor(
-                out=o_sb[u][:],
-                in0=o_ps[u][:],
-                in1=inverse[:].unsqueeze(2).to_broadcast([P, TILES_PER_UNIT, DH]),
-                op=ALU.mult,
+            o_ps[u] = psum_mx.tile([P, PIXELS], F32, name="o_ps", tag="mx")
+            nc.tensor.matmul_mx(
+                out=o_ps[u][:],
+                lhsT=q_codes[u][:].bitcast(FP8X4),
+                lhsT_scale=q_scales[u][:],
+                rhs=e_codes[u][:].bitcast(FP8X4),
+                rhs_scale=e_scales[u][:],
+                start=True,
+                stop=True,
             )
 
-        def transpose_o(u):
-            o_t[u] = psum_o.tile([P, TILES_PER_UNIT, P], F32, name="o_t", tag="o_t")
-            for mt in range(TILES_PER_UNIT):
-                nc.tensor.transpose(out=o_t[u][:, mt, :], in_=o_sb[u][:, mt, :], identity=ident_f32[:])
+        def invert(u):
+            inverse[u] = work.tile([P, TILES_PER_UNIT], F32, name="inverse", bufs=3)
+            nc.vector.reciprocal(out=inverse[u][:], in_=row_sum[u][:])
 
-        def store(u):
+        def spread_inverse(u):
+            spread_ps = psum_o.tile([P, PIXELS], F32, name="spread_ps", tag="spread")
+            for mt in range(TILES_PER_UNIT):
+                nc.tensor.transpose(
+                    out=spread_ps[:, mt * P : (mt + 1) * P],
+                    in_=inverse[u][:, mt : mt + 1].to_broadcast([P, P]),
+                    identity=ident_f32[:],
+                )
+            spread[u] = spread_ps
+
+        def fetch_inverse(u):
+            spread_sb = work.tile([P, PIXELS], F32, name="spread_sb", bufs=4)
+            nc.scalar.copy(out=spread_sb[:], in_=spread[u][:])
+            spread[u] = spread_sb
+
+        def normalise_and_store(u):
             b, h = divmod(u, HEADS)
             result = work.tile([P, PIXELS], F32, name="result", bufs=4)
-            nc.scalar.copy(out=result[:], in_=o_t[u][:].rearrange("d mt m -> d (mt m)"))
+            nc.vector.tensor_tensor(out=result[:], in0=o_ps[u][:], in1=spread[u][:], op=ALU.mult)
             nc.sync.dma_start(out=out[b, h * DH : (h + 1) * DH].rearrange("c y x -> c (y x)"), in_=result[:])
 
+        half_images = BATCH * PASSES
+        x_ticks = {max(TILES_PER_UNIT * i, X_FIRST * (i + 1)): i for i in range(half_images)}
         with tc.manual_schedule():
+            group_x(0)
             for k in range(LAST_TICK + 1):
                 if k < TILES:
                     score_matmuls(k)
                 if 0 <= k - E_TRANSPOSE < TILES:
                     transpose_e(k - E_TRANSPOSE)
-                u = due(k, O_TRANSPOSE, UNITS)
+                u = due(k, SPREAD, UNITS)
                 if u is not None:
-                    transpose_o(u)
+                    spread_inverse(u)
                 if k == W_TICK:
                     prepare_weights()
                 u = due(k, ATTEND, UNITS)
@@ -290,21 +296,23 @@ def tile_multiheadselfattention2d_pa_t_kernel(tc, vh, zh, r_pos, x, w_q, out):
 
                 if k < TILES:
                     row_maximum(k)
-                    group_x(k)
                 if k == W_TICK + 1:
                     quantise_w()
-                i = due(k, X_QUANTISE, BATCH * PASSES)
-                if i is not None:
-                    quantise_x(i)
-                u = due(k, QUANTISE_Q, UNITS)
-                if u is not None:
-                    quantise_q(u)
-                u = due(k, NORMALISE, UNITS)
-                if u is not None:
-                    normalise(u)
-                u = due(k, QUANTISE_E, UNITS)
+                u = due(k, QUANTISE, UNITS)
                 if u is not None:
                     quantise_e(u)
+                    quantise_q(u)
+                if k in x_ticks:
+                    quantise_x(x_ticks[k])
+                u = due(k, NORMALISE, UNITS)
+                if u is not None:
+                    normalise_and_store(u)
+                u = due(k, INVERT, UNITS)
+                if u is not None:
+                    invert(u)
+
+                if k in x_ticks and x_ticks[k] + 1 < half_images:
+                    group_x(x_ticks[k] + 1)
 
                 if k < TILES:
                     exponentials(k)
@@ -313,6 +321,6 @@ def tile_multiheadselfattention2d_pa_t_kernel(tc, vh, zh, r_pos, x, w_q, out):
                 u = due(k, Q_OUT, UNITS)
                 if u is not None:
                     group_q(u)
-                u = due(k, O_TRANSPOSE, UNITS)
+                u = due(k, SPREAD, UNITS)
                 if u is not None:
-                    store(u)
+                    fetch_inverse(u)

@@ -36,7 +36,7 @@ Q_OUT = 10
 INVERT = 10
 SPREAD = 11
 QUANTISE = 12
-ATTEND = 13
+ATTEND = 14
 NORMALISE = 15
 W_TICK = 6
 LAST_TICK = TILES_PER_UNIT * (UNITS - 1) + NORMALISE

@@ -25,19 +25,20 @@ PASSES = C_IN // K_PASS
 UNITS = BATCH * HEADS
 TILES_PER_UNIT = PIXELS // P
 TILES = UNITS * TILES_PER_UNIT
+HALF_IMAGES = BATCH * PASSES
 SCALE = 1.0 / math.sqrt(DH)
 
 FLOPS = 2 * BATCH * HEADS * DH * C_IN * PIXELS + 3 * 2 * UNITS * PIXELS * PIXELS * DH
 
-E_TRANSPOSE = 5
-X_FIRST = 3
-PROJECT = 9
+E_TRANSPOSE = 4
+X_QUANTISE = 4
+PROJECT = 10
 Q_OUT = 10
-INVERT = 10
-SPREAD = 11
+INVERT = 9
+SPREAD = 13
 QUANTISE = 12
-ATTEND = 14
-NORMALISE = 15
+ATTEND = 17
+NORMALISE = 18
 W_TICK = 6
 LAST_TICK = TILES_PER_UNIT * (UNITS - 1) + NORMALISE
 
@@ -159,13 +160,12 @@ def tile_multiheadselfattention2d_pa_t_kernel(tc, vh, zh, r_pos, x, w_q, out):
                 accum_out=row_sum[u][:, mt : mt + 1],
             )
 
-        def transpose_e(k):
-            pair, a = divmod(k, 2)
-            if a == 0:
-                e_t[pair] = psum_t.tile([P, 2, 2, P], F32, name="e_t", tag="e_t")
-            words = e_sb[k][:].bitcast(F32)
-            for u in range(2):
-                nc.tensor.transpose(out=e_t[pair][:, a, u, :], in_=words[:, u * P : (u + 1) * P], identity=ident_f32[:])
+        def transpose_e(pair):
+            e_t[pair] = psum_t.tile([P, 2, 2, P], F32, name="e_t", tag="e_t")
+            for a in range(2):
+                words = e_sb[2 * pair + a][:].bitcast(F32)
+                for w in range(2):
+                    nc.tensor.transpose(out=e_t[pair][:, a, w, :], in_=words[:, w * P : (w + 1) * P], identity=ident_f32[:])
 
         def group_e(pair):
             u, half = divmod(pair, 2)
@@ -273,15 +273,15 @@ def tile_multiheadselfattention2d_pa_t_kernel(tc, vh, zh, r_pos, x, w_q, out):
             nc.vector.tensor_tensor(out=result[:], in0=o_ps[u][:], in1=spread[u][:], op=ALU.mult)
             nc.sync.dma_start(out=out[b, h * DH : (h + 1) * DH].rearrange("c y x -> c (y x)"), in_=result[:])
 
-        half_images = BATCH * PASSES
-        x_ticks = {max(TILES_PER_UNIT * i, X_FIRST * (i + 1)): i for i in range(half_images)}
         with tc.manual_schedule():
             group_x(0)
             for k in range(LAST_TICK + 1):
                 if k < TILES:
                     score_matmuls(k)
-                if 0 <= k - E_TRANSPOSE < TILES:
-                    transpose_e(k - E_TRANSPOSE)
+                pair, a = divmod(k - E_TRANSPOSE, 2)
+                pair_due = a == 1 and 0 <= pair < TILES // 2
+                if pair_due:
+                    transpose_e(pair)
                 u = due(k, SPREAD, UNITS)
                 if u is not None:
                     spread_inverse(u)
@@ -302,8 +302,9 @@ def tile_multiheadselfattention2d_pa_t_kernel(tc, vh, zh, r_pos, x, w_q, out):
                 if u is not None:
                     quantise_e(u)
                     quantise_q(u)
-                if k in x_ticks:
-                    quantise_x(x_ticks[k])
+                i = due(k, X_QUANTISE, HALF_IMAGES)
+                if i is not None:
+                    quantise_x(i)
                 u = due(k, NORMALISE, UNITS)
                 if u is not None:
                     normalise_and_store(u)
@@ -311,13 +312,13 @@ def tile_multiheadselfattention2d_pa_t_kernel(tc, vh, zh, r_pos, x, w_q, out):
                 if u is not None:
                     invert(u)
 
-                if k in x_ticks and x_ticks[k] + 1 < half_images:
-                    group_x(x_ticks[k] + 1)
+                if i is not None and i + 1 < HALF_IMAGES:
+                    group_x(i + 1)
 
                 if k < TILES:
                     exponentials(k)
-                if 0 <= k - E_TRANSPOSE < TILES and (k - E_TRANSPOSE) % 2 == 1:
-                    group_e((k - E_TRANSPOSE) // 2)
+                if pair_due:
+                    group_e(pair)
                 u = due(k, Q_OUT, UNITS)
                 if u is not None:
                     group_q(u)

@@ -32,13 +32,13 @@ FLOPS = 2 * BATCH * HEADS * DH * C_IN * PIXELS + 3 * 2 * UNITS * PIXELS * PIXELS
 
 E_TRANSPOSE = 4
 X_QUANTISE = 4
-PROJECT = 10
-Q_OUT = 10
-INVERT = 9
+PROJECT = 12
+Q_OUT = 12
+INVERT = 8
 SPREAD = 13
-QUANTISE = 12
-ATTEND = 17
-NORMALISE = 18
+QUANTISE = 16
+ATTEND = 20
+NORMALISE = 21
 W_TICK = 6
 LAST_TICK = TILES_PER_UNIT * (UNITS - 1) + NORMALISE
 

@@ -32,8 +32,8 @@ FLOPS = 2 * BATCH * HEADS * DH * C_IN * PIXELS + 3 * 2 * UNITS * PIXELS * PIXELS
 
 E_TRANSPOSE = 4
 X_QUANTISE = 4
-PROJECT = 12
-Q_OUT = 12
+PROJECT = 10
+Q_OUT = 10
 INVERT = 8
 SPREAD = 13
 QUANTISE = 16
@@ -298,13 +298,17 @@ def tile_multiheadselfattention2d_pa_t_kernel(tc, vh, zh, r_pos, x, w_q, out):
                     row_maximum(k)
                 if k == W_TICK + 1:
                     quantise_w()
+                i = due(k, X_QUANTISE, HALF_IMAGES)
                 u = due(k, QUANTISE, UNITS)
-                if u is not None:
+                if i is not None:
+                    if u is not None:
+                        quantise_q(u)
+                    quantise_x(i)
+                    if u is not None:
+                        quantise_e(u)
+                elif u is not None:
                     quantise_e(u)
                     quantise_q(u)
-                i = due(k, X_QUANTISE, HALF_IMAGES)
-                if i is not None:
-                    quantise_x(i)
                 u = due(k, NORMALISE, UNITS)
                 if u is not None:
                     normalise_and_store(u)

from contextlib import ExitStack
import math

import concourse.mybir as mybir
from concourse.masks import make_identity

F32 = mybir.dt.float32
BF16 = mybir.dt.bfloat16
U32 = mybir.dt.uint32
U8 = mybir.dt.uint8
FP8X4 = mybir.dt.float8_e4m3fn_x4
ALU = mybir.AluOpType
FUNC = mybir.ActivationFunctionType

P = 128
PACK = 4
K_PASS = P * PACK

BATCH = 8
HEADS = 2
DH = 128
PIXELS = 512
C_IN = 1024
PASSES = C_IN // K_PASS
UNITS = BATCH * HEADS
TILES_PER_UNIT = PIXELS // P
TILES = UNITS * TILES_PER_UNIT
HALF_IMAGES = BATCH * PASSES
SCALE = 1.0 / math.sqrt(DH)

FLOPS = 2 * BATCH * HEADS * DH * C_IN * PIXELS + 3 * 2 * UNITS * PIXELS * PIXELS * DH

E_TRANSPOSE = 4
X_QUANTISE = 4
PROJECT = 10
Q_OUT = 10
INVERT = 8
SPREAD = 13
QUANTISE = 16
ATTEND = 20
NORMALISE = 21
W_TICK = 6
LAST_TICK = TILES_PER_UNIT * (UNITS - 1) + NORMALISE


def due(k, lag, count):
    i, phase = divmod(k - lag, TILES_PER_UNIT)
    if phase == 0 and 0 <= i < count:
        return i
    return None


def tile_multiheadselfattention2d_pa_t_kernel(tc, vh, zh, r_pos, x, w_q, out):
    nc = tc.nc
    with ExitStack() as ctx:
        const = ctx.enter_context(tc.tile_pool(name="const", bufs=1))
        inputs = ctx.enter_context(tc.tile_pool(name="inputs", bufs=BATCH))
        work = ctx.enter_context(tc.tile_pool(name="work", bufs=2))
        psum_s = ctx.enter_context(tc.psum_pool(name="psum_s", bufs=3))
        psum_t = ctx.enter_context(tc.psum_pool(name="psum_t", bufs=2))
        psum_mx = ctx.enter_context(tc.psum_pool(name="psum_mx", bufs=2))
        psum_o = ctx.enter_context(tc.psum_pool(name="psum_o", bufs=1))

        v_sb = []
        z_sb = []
        x_sb = []
        r_sb = const.tile([P, HEADS, PIXELS], BF16, name="r_sb")
        w_sb = const.tile([P, HEADS, C_IN], BF16, name="w_sb")
        for b in range(BATCH):
            v_sb.append(inputs.tile([P, HEADS, PIXELS], BF16, name="v_sb"))
            z_sb.append(inputs.tile([P, HEADS, PIXELS], BF16, name="z_sb"))
            x_sb.append(inputs.tile([P, PASSES, PACK, PIXELS], BF16, name="x_sb"))
            for h in range(HEADS):
                nc.sync.dma_start(out=v_sb[b][:, h, :], in_=vh[b, h])
                nc.sync.dma_start(out=z_sb[b][:, h, :], in_=zh[b, h])
                if b == 0:
                    nc.sync.dma_start(out=r_sb[:, h, :], in_=r_pos[h])
                nc.sync.dma_start(
                    out=x_sb[b][:, h],
                    in_=x[b, h * K_PASS : (h + 1) * K_PASS].rearrange("(p j) y x -> p j (y x)", j=PACK),
                )
            if b == 0:
                nc.sync.dma_start(out=w_sb[:], in_=w_q.rearrange("(h c) k -> c h k", h=HEADS))

        ident_f32 = const.tile([P, P], F32, name="ident_f32")
        make_identity(nc, ident_f32[:])

        w_pairs = const.tile([P, PASSES, HEADS, DH, 2], F32, name="w_pairs", align_bytes=64)
        w_codes = const.tile([P, PASSES, HEADS, DH], U32, name="w_codes", align_bytes=64)
        w_scales = const.tile([P, PASSES, HEADS, DH], U8, name="w_scales", align_bytes=64)

        s_ps = {}
        neg_s = {}
        neg_max = {}
        e_sb = {}
        e_t = {}
        e_grouped = {}
        e_codes = {}
        e_scales = {}
        row_sum = {}
        x_grouped = {}
        x_codes = {}
        x_scales = {}
        q_ps = {}
        q_grouped = {}
        q_codes = {}
        q_scales = {}
        inverse = {}
        spread = {}
        o_ps = {}

        def prepare_weights():
            for h in range(HEADS):
                words = w_sb[:, h, :].bitcast(F32).rearrange("c (g p u) -> c g u p", g=PASSES, u=2)
                w_t = psum_mx.tile([P, PASSES, 2, DH], F32, name="w_t", tag="mx")
                for g in range(PASSES):
                    for u in range(2):
                        nc.tensor.transpose(out=w_t[:, g, u, :], in_=words[:, g, u, :], identity=ident_f32[:])
                nc.vector.tensor_copy(out=w_pairs[:, :, h, :, :], in_=w_t[:].rearrange("p g u c -> p g c u"))

        def quantise_w():
            nc.vector.quantize_mx(
                out=w_codes[:].rearrange("p g h c -> p (g h c)").bitcast(FP8X4),
                scales=w_scales[:].rearrange("p g h c -> p (g h c)"),
                in_=w_pairs[:].rearrange("p g h c u -> p (g h c u)").bitcast(BF16),
            )

        def score_matmuls(k):
            u, mt = divmod(k, TILES_PER_UNIT)
            b, h = divmod(u, HEADS)
            s_ps[k] = psum_s.tile([P, PIXELS], F32, name="s_ps", tag="s")
            queries = v_sb[b][:, h, mt * P : (mt + 1) * P]
            nc.tensor.matmul(out=s_ps[k][:], lhsT=queries, rhs=z_sb[b][:, h, :], start=True, stop=False)
            nc.tensor.matmul(out=s_ps[k][:], lhsT=queries, rhs=r_sb[:, h, :], start=False, stop=True)

        def row_maximum(k):
            neg_s[k] = work.tile([P, PIXELS], F32, name="neg_s", bufs=8)
            neg_max[k] = work.tile([P, 1], F32, name="neg_max", bufs=10)
            nc.vector.tensor_scalar(
                out=neg_s[k][:],
                in0=s_ps[k][:],
                scalar1=-SCALE,
                scalar2=None,
                op0=ALU.mult,
                op1=ALU.min,
                accum_out=neg_max[k][:],
            )

        def exponentials(k):
            u, mt = divmod(k, TILES_PER_UNIT)
            if mt == 0:
                row_sum[u] = work.tile([P, TILES_PER_UNIT], F32, name="row_sum", bufs=8)
            e_sb[k] = work.tile([P, PIXELS], BF16, name="e_sb", bufs=8)
            nc.scalar.activation(
                out=e_sb[k][:].rearrange("m (u p e) -> m u p e", u=2, e=2),
                in_=neg_s[k][:].rearrange("m (u e p) -> m u p e", u=2, e=2),
                func=FUNC.Exp,
                bias=neg_max[k][:],
                scale=-1.0,
                accum_out=row_sum[u][:, mt : mt + 1],
            )

        def transpose_e(pair):
            e_t[pair] = psum_t.tile([P, 2, 2, P], F32, name="e_t", tag="e_t")
            for a in range(2):
                words = e_sb[2 * pair + a][:].bitcast(F32)
                for w in range(2):
                    nc.tensor.transpose(out=e_t[pair][:, a, w, :], in_=words[:, w * P : (w + 1) * P], identity=ident_f32[:])

        def group_e(pair):
            u, half = divmod(pair, 2)
            if half == 0:
                e_grouped[u] = work.tile([P, PIXELS, 2], F32, name="e_grouped", bufs=4, align_bytes=64)
            nc.scalar.copy(
                out=e_grouped[u][:, half * 2 * P : (half + 1) * 2 * P, :].rearrange("p (a r) w -> p a r w", a=2),
                in_=e_t[pair][:].rearrange("p a w r -> p a r w"),
            )

        def quantise_e(u):
            e_codes[u] = work.tile([P, PIXELS], U32, name="e_codes", bufs=4, align_bytes=64)
            e_scales[u] = work.tile([P, PIXELS], U8, name="e_scales", bufs=4, align_bytes=64)
            nc.vector.quantize_mx(
                out=e_codes[u][:].bitcast(FP8X4),
                scales=e_scales[u][:],
                in_=e_grouped[u][:].rearrange("p m w -> p (m w)").bitcast(BF16),
            )

        def group_x(half_image):
            b, g = divmod(half_image, PASSES)
            x_grouped[half_image] = work.tile([P, PIXELS, PACK], BF16, name="x_grouped", bufs=1, align_bytes=64)
            nc.gpsimd.tensor_scalar(
                out=x_grouped[half_image][:],
                in0=x_sb[b][:, g].rearrange("p j n -> p n j"),
                scalar1=1.0,
                scalar2=0.0,
                op0=ALU.mult,
                op1=ALU.add,
            )

        def quantise_x(half_image):
            b, g = divmod(half_image, PASSES)
            if g == 0:
                x_codes[b] = work.tile([P, PASSES, PIXELS], U32, name="x_codes", bufs=3, align_bytes=64)
                x_scales[b] = work.tile([P, PASSES, PIXELS], U8, name="x_scales", bufs=3, align_bytes=64)
            nc.vector.quantize_mx(
                out=x_codes[b][:, g, :].bitcast(FP8X4),
                scales=x_scales[b][:, g, :],
                in_=x_grouped[half_image][:].rearrange("p n j -> p (n j)"),
            )

        def project(u):
            b, h = divmod(u, HEADS)
            q_ps[u] = psum_mx.tile([P, PACK, DH], F32, name="q_ps", tag="mx")
            for t in range(PACK):
                for g in range(PASSES):
                    nc.tensor.matmul_mx(
                        out=q_ps[u][:, t, :],
                        lhsT=x_codes[b][:, g, t * P : (t + 1) * P].bitcast(FP8X4),
                        lhsT_scale=x_scales[b][:, g, t * P : (t + 1) * P],
                        rhs=w_codes[:, g, h, :].bitcast(FP8X4),
                        rhs_scale=w_scales[:, g, h, :],
                        start=(g == 0),
                        stop=(g == PASSES - 1),
                    )

        def group_q(u):
            q_grouped[u] = work.tile([P, DH, PACK], BF16, name="q_grouped", bufs=2, align_bytes=64)
            nc.scalar.copy(out=q_grouped[u][:], in_=q_ps[u][:].rearrange("p t d -> p d t"))

        def quantise_q(u):
            q_codes[u] = work.tile([P, DH], U32, name="q_codes", bufs=3, align_bytes=64)
            q_scales[u] = work.tile([P, DH], U8, name="q_scales", bufs=3, align_bytes=64)
            nc.vector.quantize_mx(
                out=q_codes[u][:].bitcast(FP8X4),
                scales=q_scales[u][:],
                in_=q_grouped[u][:].rearrange("p d t -> p (d t)"),
            )

        def attend(u):
            o_ps[u] = psum_mx.tile([P, PIXELS], F32, name="o_ps", tag="mx")
            nc.tensor.matmul_mx(
                out=o_ps[u][:],
                lhsT=q_codes[u][:].bitcast(FP8X4),
                lhsT_scale=q_scales[u][:],
                rhs=e_codes[u][:].bitcast(FP8X4),
                rhs_scale=e_scales[u][:],
                start=True,
                stop=True,
            )

        def invert(u):
            inverse[u] = work.tile([P, TILES_PER_UNIT], F32, name="inverse", bufs=3)
            nc.vector.reciprocal(out=inverse[u][:], in_=row_sum[u][:])

        def spread_inverse(u):
            spread_ps = psum_o.tile([P, PIXELS], F32, name="spread_ps", tag="spread")
            for mt in range(TILES_PER_UNIT):
                nc.tensor.transpose(
                    out=spread_ps[:, mt * P : (mt + 1) * P],
                    in_=inverse[u][:, mt : mt + 1].to_broadcast([P, P]),
                    identity=ident_f32[:],
                )
            spread[u] = spread_ps

        def fetch_inverse(u):
            spread_sb = work.tile([P, PIXELS], F32, name="spread_sb", bufs=4)
            nc.scalar.copy(out=spread_sb[:], in_=spread[u][:])
            spread[u] = spread_sb

        def normalise_and_store(u):
            b, h = divmod(u, HEADS)
            result = work.tile([P, PIXELS], F32, name="result", bufs=4)
            nc.vector.tensor_tensor(out=result[:], in0=o_ps[u][:], in1=spread[u][:], op=ALU.mult)
            nc.sync.dma_start(out=out[b, h * DH : (h + 1) * DH].rearrange("c y x -> c (y x)"), in_=result[:])

        with tc.manual_schedule():
            group_x(0)
            for k in range(LAST_TICK + 1):
                if k < TILES:
                    score_matmuls(k)
                pair, a = divmod(k - E_TRANSPOSE, 2)
                pair_due = a == 1 and 0 <= pair < TILES // 2
                if pair_due:
                    transpose_e(pair)
                u = due(k, SPREAD, UNITS)
                if u is not None:
                    spread_inverse(u)
                if k == W_TICK:
                    prepare_weights()
                u = due(k, ATTEND, UNITS)
                if u is not None:
                    attend(u)
                u = due(k, PROJECT, UNITS)
                if u is not None:
                    project(u)

                if k < TILES:
                    row_maximum(k)
                if k == W_TICK + 1:
                    quantise_w()
                i = due(k, X_QUANTISE, HALF_IMAGES)
                u = due(k, QUANTISE, UNITS)
                if i is not None:
                    if u is not None:
                        quantise_q(u)
                    quantise_x(i)
                    if u is not None:
                        quantise_e(u)
                elif u is not None:
                    quantise_e(u)
                    quantise_q(u)
                u = due(k, NORMALISE, UNITS)
                if u is not None:
                    normalise_and_store(u)
                u = due(k, INVERT, UNITS)
                if u is not None:
                    invert(u)

                if i is not None and i + 1 < HALF_IMAGES:
                    group_x(i + 1)

                if k < TILES:
                    exponentials(k)
                if pair_due:
                    group_e(pair)
                u = due(k, Q_OUT, UNITS)
                if u is not None:
                    group_q(u)
                u = due(k, SPREAD, UNITS)
                if u is not None:
                    fetch_inverse(u)
